import numpy as np
import ml_dtypes


def mxq(x, axis, fmt="e4m3"):
    dtype, down = {"e4m3": (ml_dtypes.float8_e4m3fn, 7), "e5m2": (ml_dtypes.float8_e5m2, 14)}[fmt]
    v = np.moveaxis(np.asarray(x, np.float32).astype(ml_dtypes.bfloat16).astype(np.float64), axis, -1)
    blocks = v.reshape(v.shape[:-1] + (-1, 32))
    amax = np.abs(blocks).max(-1, keepdims=True)
    byte = np.maximum(np.where(amax > 0, np.frexp(amax)[1] - 1 + 127, 0) - down, 1)
    scale = np.exp2(byte - 127.0)
    codes = (blocks / scale).astype(np.float32).astype(dtype).astype(np.float64)
    return np.moveaxis((codes * scale).reshape(v.shape), -1, axis)


WIDE = False


def mx_kscale(k):
    if not WIDE:
        return np.ones(k)
    levels = np.array([10, -10, 5, -5, 0])
    a = np.random.permutation(np.resize(levels, k // 512 * 4)).reshape(k // 512, 4)
    idx = np.arange(k)
    return np.exp2(a[idx // 512, idx % 128 // 32])


BF16 = ml_dtypes.bfloat16


def bf(x):
    return np.asarray(x, np.float32).astype(BF16)


def f64(x):
    return np.asarray(x).astype(np.float64)


B, C, T, H = 4, 512, 2048, 256
EPS_LN = 1e-5
EPS_STD = 1e-5


def ln_dim1(z, g, b):
    mu = z.mean(axis=1, keepdims=True)
    var = ((z - mu) ** 2).mean(axis=1, keepdims=True)
    return (z - mu) / np.sqrt(var + EPS_LN) * g[None, :, None] + b[None, :, None]


def stats(x, m):
    mean = (m * x).sum(axis=2)
    std = np.sqrt(np.maximum((m * x * x).sum(axis=2) - mean ** 2, EPS_STD))
    return mean, std


def setup_inputs():
    s = mx_kscale(C)
    lens = np.random.randint(T // 2, T, size=B)
    mask = (np.arange(T)[None, None, :] < lens[:, None, None]) * 1.0
    off = 0.5 * np.random.standard_normal((B, C, 1))
    gain = 0.5 + np.random.random((B, C, 1))
    pad = np.random.standard_normal((B, C, 1)) * (1.0 - mask)
    x = off + gain * np.random.standard_normal((B, C, T)) + pad
    return {"x": bf(x * s[None, :, None]),
            "mask": bf(mask),
            "w1": bf(np.random.standard_normal((H, 3 * C)) / np.sqrt(3 * C) / np.tile(s, 3)[None, :]),
            "b1": bf(0.1 * np.random.standard_normal(H)),
            "g1": bf(1.0 + 0.1 * np.random.standard_normal(H)),
            "be1": bf(0.1 * np.random.standard_normal(H))}


def reference(x, mask, w1, b1, g1, be1):
    x, mask = f64(x), f64(mask)
    total = mask.sum(axis=2, keepdims=True)
    mean0, std0 = stats(x, mask / total)
    mean0 = mean0
    std0 = std0
    x_in = np.concatenate([
        x,
        np.broadcast_to(mean0[:, :, None], (B, C, T)),
        np.broadcast_to(std0[:, :, None], (B, C, T)),
    ], axis=1)
    u = (mxq(f64(w1), 1, "e4m3") @ mxq(x_in, 1, "e4m3")) + f64(b1)[None, :, None]
    return np.tanh(ln_dim1(np.maximum(u, 0.0), f64(g1), f64(be1)))

@@ -1,0 +1,244 @@
+from contextlib import ExitStack
+
+import concourse.mybir as mybir
+from concourse.masks import make_identity
+
+F32 = mybir.dt.float32
+BF16 = mybir.dt.bfloat16
+U32 = mybir.dt.uint32
+U8 = mybir.dt.uint8
+FP8X4 = mybir.dt.float8_e4m3fn_x4
+ALU = mybir.AluOpType
+ACT = mybir.ActivationFunctionType
+AX = mybir.AxisListType
+
+B, C, T, H = 4, 512, 2048, 256
+P = 128
+PACK = 4
+CHUNK = 512
+NCH = T // CHUNK
+TILES = CHUNK // P
+EPS_LN = 1e-5
+EPS_STD = 1e-5
+LEAD = 6
+FLOPS = 2 * B * H * 3 * C * T
+
+
+def tile_attentivestatspool_pa_t_kernel(tc, x, mask, w1, b1, g1, be1, out):
+    nc = tc.nc
+    with ExitStack() as ctx:
+        const = ctx.enter_context(tc.tile_pool(name="const", bufs=1))
+        xmp = ctx.enter_context(tc.tile_pool(name="xmp", bufs=3))
+        grp = ctx.enter_context(tc.tile_pool(name="grp", bufs=3))
+        cod = ctx.enter_context(tc.tile_pool(name="cod", bufs=3))
+        sml = ctx.enter_context(tc.tile_pool(name="sml", bufs=6))
+        per = ctx.enter_context(tc.tile_pool(name="per", bufs=2))
+        up = ctx.enter_context(tc.tile_pool(name="up", bufs=5))
+        zp = ctx.enter_context(tc.tile_pool(name="zp", bufs=3))
+        op = ctx.enter_context(tc.tile_pool(name="op", bufs=3))
+        ps_mx = ctx.enter_context(tc.psum_pool(name="ps_mx", bufs=4))
+        ps_tr = ctx.enter_context(tc.psum_pool(name="ps_tr", bufs=3))
+        ps_ms = ctx.enter_context(tc.psum_pool(name="ps_ms", bufs=1))
+
+        raw = []
+        mbc = []
+        for b in range(B):
+            raw.append(const.tile([P, PACK, T], BF16, name="raw%d" % b))
+            mbc.append(const.tile([P, T], BF16, name="mbc%d" % b))
+        mask_rows = mask.rearrange("b o t -> (b o) t")
+        x_v = [x[b].rearrange("(p j) t -> p j t", j=PACK) for b in range(B)]
+        for s in range(NCH):
+            nc.sync.dma_start(out=raw[0][:, :, s * CHUNK:(s + 1) * CHUNK],
+                              in_=x_v[0][:, :, s * CHUNK:(s + 1) * CHUNK])
+        for b in range(1, B):
+            nc.sync.dma_start(out=raw[b][:], in_=x_v[b])
+
+        msk = const.tile([P, T * B // P], BF16, name="msk")
+        w1_sb = const.tile([P, 2, 3 * C], BF16, name="w1_sb")
+        b1bc = const.tile([P, H], BF16, name="b1bc")
+        pr = const.tile([P, P], BF16, name="pr")
+        nc.vector.memset(pr[:], 0.0)
+        nc.scalar.dma_start(out=mbc[0][:], in_=mask_rows[0].partition_broadcast(P))
+        nc.scalar.dma_start(out=msk[:], in_=mask.rearrange("b o (r f) -> (b o r) f", f=T * B // P))
+        nc.scalar.dma_start(out=w1_sb[:], in_=w1.rearrange("(hh p) k -> p hh k", p=P))
+        nc.scalar.dma_start(out=b1bc[:], in_=b1.partition_broadcast(P))
+        nc.scalar.dma_start(out=mbc[1][:], in_=mask_rows[1].partition_broadcast(P))
+        nc.scalar.dma_start(out=pr[0:2, :], in_=g1.rearrange("(r f) -> r f", f=P))
+        nc.scalar.dma_start(out=pr[2:4, :], in_=be1.rearrange("(r f) -> r f", f=P))
+        nc.scalar.dma_start(out=mbc[2][:], in_=mask_rows[2].partition_broadcast(P))
+        nc.scalar.dma_start(out=mbc[3][:], in_=mask_rows[3].partition_broadcast(P))
+
+        ident_f = const.tile([P, P], F32, name="ident_f")
+        make_identity(nc, ident_f[:])
+        ident_b = const.tile([P, P], BF16, name="ident_b")
+        make_identity(nc, ident_b[:])
+        ones_f = const.tile([P, P], F32, name="ones_f")
+        nc.vector.memset(ones_f[:], 1.0)
+        half = const.tile([P, PACK], F32, name="half")
+        nc.vector.memset(half[:], 0.5)
+        nhalf = const.tile([P, TILES], F32, name="nhalf")
+        nc.vector.memset(nhalf[:], -0.5)
+
+        w1c = const.tile([P, 3, H], U32, name="w1c", align_bytes=64)
+        w1s = const.tile([P, 3, H], U8, name="w1s", align_bytes=64)
+        gb = const.tile([P, 4], F32, name="gb")
+        r_t = const.tile([P, B], F32, name="r_t")
+
+        def totals_and_params():
+            part = const.tile([P, 1], F32, name="part")
+            nc.vector.tensor_reduce(out=part[:], in_=msk[:], axis=AX.X, op=ALU.add)
+            ind = const.tile([P, 32], F32, name="ind")
+            nc.vector.memset(ind[:], 0.0)
+            nc.vector.tensor_reduce(out=ind[:, 0:B], in_=ident_f[:].rearrange("p (b q) -> p b q", b=B),
+                                    axis=AX.X, op=ALU.add)
+            rhs_tot = const.tile([P, 32], F32, name="rhs_tot")
+            nc.vector.tensor_scalar(out=rhs_tot[:], in0=ind[:], scalar1=part[:, 0:1], scalar2=None, op0=ALU.mult)
+            ps_tot = ps_ms.tile([P, 32], F32, tag="ms", name="ps_tot")
+            nc.tensor.matmul(out=ps_tot[:], lhsT=ones_f[:], rhs=rhs_tot[:], start=True, stop=True)
+            rtot = const.tile([P, B], F32, name="rtot")
+            nc.vector.reciprocal(out=rtot[:], in_=ps_tot[:, 0:B])
+            nc.vector.tensor_scalar(out=r_t[:], in0=rtot[:], scalar1=float(T), scalar2=None, op0=ALU.mult)
+            ps_pr = ps_ms.tile([P, P], BF16, tag="ms", name="ps_pr")
+            nc.tensor.transpose(out=ps_pr[:], in_=pr[:], identity=ident_b[:])
+            nc.vector.tensor_copy(out=gb[:], in_=ps_pr[:, 0:4])
+
+        def w1_prep():
+            w1p = const.tile([P, 2, 3, PACK, P], BF16, name="w1p")
+            w1g = const.tile([P, 3, H, PACK], BF16, name="w1g", align_bytes=64)
+            nc.vector.tensor_copy(out=w1p[:, 0], in_=w1_sb[:, 0, :].rearrange("p (g q j) -> p g j q", g=3, j=PACK))
+            nc.scalar.copy(out=w1p[:, 1], in_=w1_sb[:, 1, :].rearrange("p (g q j) -> p g j q", g=3, j=PACK))
+            for g in range(3):
+                pw = ps_tr.tile([P, PACK, H], BF16, tag="tr", name="pw")
+                for hh in range(2):
+                    for j in range(PACK):
+                        nc.tensor.transpose(out=pw[:, j, hh * P:(hh + 1) * P], in_=w1p[:, hh, g, j, :],
+                                            identity=ident_b[:])
+                nc.vector.tensor_copy(out=w1g[:, g], in_=pw[:].rearrange("q j h -> q h j"))
+            for g in range(3):
+                nc.vector.quantize_mx(out=w1c[:, g, :].bitcast(FP8X4), scales=w1s[:, g, :],
+                                      in_=w1g[:, g].rearrange("q h j -> q (h j)"))
+
+        xc = {}
+        xs = {}
+        st = {}
+        vb = {}
+
+        def front_chunk(f):
+            b, s = divmod(f, NCH)
+            cols = slice(s * CHUNK, (s + 1) * CHUNK)
+            if s == 0:
+                xc[b] = cod.tile([P, T], U32, name="xc", align_bytes=64)
+                xs[b] = cod.tile([P, T], U8, name="xs", align_bytes=64)
+                st[b] = per.tile([P, PACK, NCH, 6], F32, name="st")
+            xm = xmp.tile([P, PACK, CHUNK], BF16, name="xm")
+            nc.vector.tensor_tensor(out=xm[:], in0=raw[b][:, :, cols],
+                                    in1=mbc[b][:, cols].unsqueeze(1).to_broadcast([P, PACK, CHUNK]), op=ALU.mult)
+            for j in range(PACK):
+                nc.vector.bn_stats(out=st[b][:, j, s, :], in_=xm[:, j, :])
+            grouped = grp.tile([P, CHUNK, PACK], BF16, name="grouped", align_bytes=64)
+            nc.scalar.copy(out=grouped[:].rearrange("p (c i) j -> p c j i", i=4),
+                           in_=raw[b][:, :, cols].rearrange("p j (c i) -> p c j i", i=4))
+            nc.vector.quantize_mx(out=xc[b][:, cols].bitcast(FP8X4), scales=xs[b][:, cols],
+                                  in_=grouped[:].rearrange("p w j -> p (w j)"))
+            if s == NCH - 1:
+                front_finish(b)
+
+        def front_finish(b):
+            mv = per.tile([P, PACK, 2], F32, name="mv")
+            for j in range(PACK):
+                nc.vector.bn_aggr(out=mv[:, j, :], in_=st[b][:, j].rearrange("p s k -> p (s k)"))
+            mean = mv[:, :, 0]
+            var = mv[:, :, 1]
+            rb = r_t[:, b:b + 1]
+            ms = per.tile([P, 2, PACK], F32, name="ms")
+            d = per.tile([P, PACK], F32, name="d")
+            t1 = per.tile([P, PACK], F32, name="t1")
+            vr = per.tile([P, PACK], F32, name="vr")
+            nc.gpsimd.tensor_scalar(out=ms[:, 0, :], in0=mean, scalar1=rb, scalar2=0.0, op0=ALU.mult, op1=ALU.add)
+            nc.gpsimd.tensor_tensor(out=d[:], in0=mean, in1=ms[:, 0, :], op=ALU.subtract)
+            nc.gpsimd.tensor_tensor(out=t1[:], in0=ms[:, 0, :], in1=d[:], op=ALU.mult)
+            nc.gpsimd.tensor_scalar(out=vr[:], in0=var, scalar1=rb, scalar2=0.0, op0=ALU.mult, op1=ALU.add)
+            nc.gpsimd.tensor_tensor(out=vr[:], in0=vr[:], in1=t1[:], op=ALU.add)
+            nc.gpsimd.tensor_scalar(out=vr[:], in0=vr[:], scalar1=EPS_STD, scalar2=None, op0=ALU.max)
+            nc.gpsimd.tensor_tensor(out=ms[:, 1, :], in0=vr[:], in1=half[:], op=ALU.pow)
+            msb = per.tile([P, 2, P, PACK], BF16, name="msb", align_bytes=64)
+            nc.gpsimd.tensor_scalar(out=msb[:], in0=ms[:].unsqueeze(2).to_broadcast([P, 2, P, PACK]),
+                                    scalar1=1.0, scalar2=0.0, op0=ALU.mult, op1=ALU.add)
+            mc = per.tile([P, 2 * P], U32, name="mc", align_bytes=64)
+            msc = per.tile([P, 2 * P], U8, name="msc", align_bytes=64)
+            nc.vector.quantize_mx(out=mc[:].bitcast(FP8X4), scales=msc[:],
+                                  in_=msb[:].rearrange("p g w j -> p (g w j)"))
+            ps_vb = ps_ms.tile([P, H], F32, tag="ms", name="ps_vb")
+            for gi in range(2):
+                nc.tensor.matmul_mx(out=ps_vb[:], lhsT=mc[:, gi * P:(gi + 1) * P].bitcast(FP8X4),
+                                    lhsT_scale=msc[:, gi * P:(gi + 1) * P],
+                                    rhs=w1c[:, 1 + gi, :].bitcast(FP8X4), rhs_scale=w1s[:, 1 + gi, :],
+                                    start=(gi == 0), stop=(gi == 1))
+            vb[b] = per.tile([P, H], F32, name="vb")
+            nc.vector.tensor_tensor(out=vb[b][:], in0=ps_vb[:], in1=b1bc[:], op=ALU.add)
+
+        live = {}
+
+        def stage1(g):
+            b, s = divmod(g, NCH)
+            a = up.tile([P, TILES, H], F32, name="a")
+            for pair in range(TILES // 2):
+                ps = ps_mx.tile([P, 2, H], F32, name="ps")
+                for i in range(2):
+                    t0 = s * CHUNK + (2 * pair + i) * P
+                    nc.tensor.matmul_mx(out=ps[:, i, :], lhsT=xc[b][:, t0:t0 + P].bitcast(FP8X4),
+                                        lhsT_scale=xs[b][:, t0:t0 + P],
+                                        rhs=w1c[:, 0, :].bitcast(FP8X4), rhs_scale=w1s[:, 0, :],
+                                        start=True, stop=True)
+                nc.vector.tensor_tensor(out=a[:, 2 * pair:2 * pair + 2, :], in0=ps[:],
+                                        in1=vb[b][:].unsqueeze(1).to_broadcast([P, 2, H]), op=ALU.add)
+            s1 = sml.tile([P, TILES], F32, name="s1")
+            s2 = sml.tile([P, TILES], F32, name="s2")
+            for k in range(TILES):
+                nc.scalar.activation(out=a[:, k, :], in_=a[:, k, :], func=ACT.Relu, accum_out=s1[:, k:k + 1])
+            for k in range(TILES):
+                junk = zp.tile([P, H], F32, name="junk")
+                nc.scalar.activation(out=junk[:], in_=a[:, k, :], func=ACT.Square, accum_out=s2[:, k:k + 1])
+            negmu = sml.tile([P, TILES], F32, name="negmu")
+            msq = sml.tile([P, TILES], F32, name="msq")
+            rstd = sml.tile([P, TILES], F32, name="rstd")
+            nc.gpsimd.tensor_scalar(out=negmu[:], in0=s1[:], scalar1=-1.0 / H, scalar2=0.0, op0=ALU.mult, op1=ALU.add)
+            nc.gpsimd.tensor_tensor(out=msq[:], in0=negmu[:], in1=negmu[:], op=ALU.mult)
+            nc.gpsimd.tensor_scalar(out=s2[:], in0=s2[:], scalar1=1.0 / H, scalar2=0.0, op0=ALU.mult, op1=ALU.add)
+            nc.gpsimd.tensor_tensor(out=msq[:], in0=s2[:], in1=msq[:], op=ALU.subtract)
+            nc.gpsimd.tensor_scalar(out=msq[:], in0=msq[:], scalar1=0.0, scalar2=EPS_LN, op0=ALU.max, op1=ALU.add)
+            nc.gpsimd.tensor_tensor(out=rstd[:], in0=msq[:], in1=nhalf[:], op=ALU.pow)
+            live[g] = (a, negmu, rstd)
+
+        def stage2(g):
+            b, s = divmod(g, NCH)
+            a, negmu, rstd = live.pop(g)
+            zh = zp.tile([P, TILES, H], F32, name="zh")
+            for k in range(TILES):
+                nc.vector.tensor_scalar(out=zh[:, k, :], in0=a[:, k, :], scalar1=negmu[:, k:k + 1],
+                                        scalar2=rstd[:, k:k + 1], op0=ALU.add, op1=ALU.mult)
+            o = op.tile([P, 2, CHUNK], F32, name="o")
+            for hh in range(2):
+                pt = ps_tr.tile([P, CHUNK], F32, tag="tr", name="pt")
+                for k in range(TILES):
+                    nc.tensor.transpose(out=pt[:, k * P:(k + 1) * P], in_=zh[:, k, hh * P:(hh + 1) * P],
+                                        identity=ident_f[:])
+                nc.scalar.activation(out=o[:, hh, :], in_=pt[:], func=ACT.Tanh,
+                                     scale=gb[:, hh:hh + 1], bias=gb[:, 2 + hh:3 + hh])
+            nc.sync.dma_start(out=out[b].rearrange("(hh p) t -> p hh t", p=P)[:, :, s * CHUNK:(s + 1) * CHUNK],
+                              in_=o[:])
+
+        n_f = B * NCH
+        front_chunk(0)
+        front_chunk(1)
+        totals_and_params()
+        w1_prep()
+        for f in range(2, LEAD):
+            front_chunk(f)
+        for g in range(n_f):
+            if g + LEAD < n_f:
+                front_chunk(g + LEAD)
+            stage1(g)
+            if g >= 1:
+                stage2(g - 1)
+        stage2(n_f - 1)

@@ -18,9 +18,14 @@ PACK = 4
 CHUNK = 512
 NCH = T // CHUNK
 TILES = CHUNK // P
+NG = B * NCH
 EPS_LN = 1e-5
 EPS_STD = 1e-5
 LEAD = 6
+PINNED = True
+NSQV = [0,0,0,0,0,0,0,0,0,0,0,0,4,4,4,4]
+P4G = [0,0,0,0,0,0,0,0,0,0,0,0,0,0,0,0]
+RGG = []
 FLOPS = 2 * B * H * 3 * C * T
 
 
@@ -33,62 +38,64 @@ def tile_attentivestatspool_pa_t_kernel(tc, x, mask, w1, b1, g1, be1, out):
         cod = ctx.enter_context(tc.tile_pool(name="cod", bufs=3))
         sml = ctx.enter_context(tc.tile_pool(name="sml", bufs=6))
         per = ctx.enter_context(tc.tile_pool(name="per", bufs=2))
-        up = ctx.enter_context(tc.tile_pool(name="up", bufs=5))
+        up = ctx.enter_context(tc.tile_pool(name="up", bufs=6))
         zp = ctx.enter_context(tc.tile_pool(name="zp", bufs=3))
         op = ctx.enter_context(tc.tile_pool(name="op", bufs=3))
         ps_mx = ctx.enter_context(tc.psum_pool(name="ps_mx", bufs=4))
         ps_tr = ctx.enter_context(tc.psum_pool(name="ps_tr", bufs=3))
         ps_ms = ctx.enter_context(tc.psum_pool(name="ps_ms", bufs=1))
+        if PINNED:
+            ctx.enter_context(tc.manual_schedule())
 
         raw = []
         mbc = []
         for b in range(B):
             raw.append(const.tile([P, PACK, T], BF16, name="raw%d" % b))
             mbc.append(const.tile([P, T], BF16, name="mbc%d" % b))
-        mask_rows = mask.rearrange("b o t -> (b o) t")
-        x_v = [x[b].rearrange("(p j) t -> p j t", j=PACK) for b in range(B)]
-        for s in range(NCH):
-            nc.sync.dma_start(out=raw[0][:, :, s * CHUNK:(s + 1) * CHUNK],
-                              in_=x_v[0][:, :, s * CHUNK:(s + 1) * CHUNK])
-        for b in range(1, B):
-            nc.sync.dma_start(out=raw[b][:], in_=x_v[b])
-
         msk = const.tile([P, T * B // P], BF16, name="msk")
         w1_sb = const.tile([P, 2, 3 * C], BF16, name="w1_sb")
         b1bc = const.tile([P, H], BF16, name="b1bc")
         pr = const.tile([P, P], BF16, name="pr")
         nc.vector.memset(pr[:], 0.0)
+        mask_rows = mask.rearrange("b o t -> (b o) t")
+        x_v = [x[b].rearrange("(p j) t -> p j t", j=PACK) for b in range(B)]
+        for s in range(NCH):
+            nc.sync.dma_start(out=raw[0][:, :, s * CHUNK:(s + 1) * CHUNK],
+                              in_=x_v[0][:, :, s * CHUNK:(s + 1) * CHUNK])
+        nc.sync.dma_start(out=w1_sb[:], in_=w1.rearrange("(hh p) k -> p hh k", p=P))
+        for b in range(1, B):
+            nc.sync.dma_start(out=raw[b][:], in_=x_v[b])
         nc.scalar.dma_start(out=mbc[0][:], in_=mask_rows[0].partition_broadcast(P))
         nc.scalar.dma_start(out=msk[:], in_=mask.rearrange("b o (r f) -> (b o r) f", f=T * B // P))
-        nc.scalar.dma_start(out=w1_sb[:], in_=w1.rearrange("(hh p) k -> p hh k", p=P))
         nc.scalar.dma_start(out=b1bc[:], in_=b1.partition_broadcast(P))
-        nc.scalar.dma_start(out=mbc[1][:], in_=mask_rows[1].partition_broadcast(P))
         nc.scalar.dma_start(out=pr[0:2, :], in_=g1.rearrange("(r f) -> r f", f=P))
         nc.scalar.dma_start(out=pr[2:4, :], in_=be1.rearrange("(r f) -> r f", f=P))
-        nc.scalar.dma_start(out=mbc[2][:], in_=mask_rows[2].partition_broadcast(P))
-        nc.scalar.dma_start(out=mbc[3][:], in_=mask_rows[3].partition_broadcast(P))
+        for b in range(1, B):
+            nc.scalar.dma_start(out=mbc[b][:], in_=mask_rows[b].partition_broadcast(P))
 
-        ident_f = const.tile([P, P], F32, name="ident_f")
-        make_identity(nc, ident_f[:])
         ident_b = const.tile([P, P], BF16, name="ident_b")
         make_identity(nc, ident_b[:])
+        ident_f = const.tile([P, P], F32, name="ident_f")
+        make_identity(nc, ident_f[:])
         ones_f = const.tile([P, P], F32, name="ones_f")
         nc.vector.memset(ones_f[:], 1.0)
         half = const.tile([P, PACK], F32, name="half")
         nc.vector.memset(half[:], 0.5)
         nhalf = const.tile([P, TILES], F32, name="nhalf")
         nc.vector.memset(nhalf[:], -0.5)
+        ind = const.tile([P, 32], F32, name="ind")
+        nc.vector.memset(ind[:], 0.0)
 
         w1c = const.tile([P, 3, H], U32, name="w1c", align_bytes=64)
         w1s = const.tile([P, 3, H], U8, name="w1s", align_bytes=64)
+        w1p = const.tile([P, 2, 3, PACK, P], BF16, name="w1p")
+        w1g = const.tile([P, 3, H, PACK], BF16, name="w1g", align_bytes=64)
         gb = const.tile([P, 4], F32, name="gb")
         r_t = const.tile([P, B], F32, name="r_t")
 
-        def totals_and_params():
+        def totals():
             part = const.tile([P, 1], F32, name="part")
             nc.vector.tensor_reduce(out=part[:], in_=msk[:], axis=AX.X, op=ALU.add)
-            ind = const.tile([P, 32], F32, name="ind")
-            nc.vector.memset(ind[:], 0.0)
             nc.vector.tensor_reduce(out=ind[:, 0:B], in_=ident_f[:].rearrange("p (b q) -> p b q", b=B),
                                     axis=AX.X, op=ALU.add)
             rhs_tot = const.tile([P, 32], F32, name="rhs_tot")
@@ -98,22 +105,26 @@ def tile_attentivestatspool_pa_t_kernel(tc, x, mask, w1, b1, g1, be1, out):
             rtot = const.tile([P, B], F32, name="rtot")
             nc.vector.reciprocal(out=rtot[:], in_=ps_tot[:, 0:B])
             nc.vector.tensor_scalar(out=r_t[:], in0=rtot[:], scalar1=float(T), scalar2=None, op0=ALU.mult)
+
+        def params():
             ps_pr = ps_ms.tile([P, P], BF16, tag="ms", name="ps_pr")
             nc.tensor.transpose(out=ps_pr[:], in_=pr[:], identity=ident_b[:])
             nc.vector.tensor_copy(out=gb[:], in_=ps_pr[:, 0:4])
 
-        def w1_prep():
-            w1p = const.tile([P, 2, 3, PACK, P], BF16, name="w1p")
-            w1g = const.tile([P, 3, H, PACK], BF16, name="w1g", align_bytes=64)
-            nc.vector.tensor_copy(out=w1p[:, 0], in_=w1_sb[:, 0, :].rearrange("p (g q j) -> p g j q", g=3, j=PACK))
-            nc.scalar.copy(out=w1p[:, 1], in_=w1_sb[:, 1, :].rearrange("p (g q j) -> p g j q", g=3, j=PACK))
+        def w1_permute():
+            for hh in range(2):
+                nc.scalar.copy(out=w1p[:, hh], in_=w1_sb[:, hh, :].rearrange("p (g q j) -> p g j q", g=3, j=PACK))
+
+        def w1_transpose():
             for g in range(3):
                 pw = ps_tr.tile([P, PACK, H], BF16, tag="tr", name="pw")
                 for hh in range(2):
                     for j in range(PACK):
                         nc.tensor.transpose(out=pw[:, j, hh * P:(hh + 1) * P], in_=w1p[:, hh, g, j, :],
                                             identity=ident_b[:])
-                nc.vector.tensor_copy(out=w1g[:, g], in_=pw[:].rearrange("q j h -> q h j"))
+                nc.scalar.copy(out=w1g[:, g], in_=pw[:].rearrange("q j h -> q h j"))
+
+        def w1_quant():
             for g in range(3):
                 nc.vector.quantize_mx(out=w1c[:, g, :].bitcast(FP8X4), scales=w1s[:, g, :],
                                       in_=w1g[:, g].rearrange("q h j -> q (h j)"))
@@ -122,28 +133,42 @@ def tile_attentivestatspool_pa_t_kernel(tc, x, mask, w1, b1, g1, be1, out):
         xs = {}
         st = {}
         vb = {}
+        gr = {}
+        fin = {}
 
-        def front_chunk(f):
+        def tt_bn(f):
             b, s = divmod(f, NCH)
             cols = slice(s * CHUNK, (s + 1) * CHUNK)
             if s == 0:
-                xc[b] = cod.tile([P, T], U32, name="xc", align_bytes=64)
-                xs[b] = cod.tile([P, T], U8, name="xs", align_bytes=64)
                 st[b] = per.tile([P, PACK, NCH, 6], F32, name="st")
             xm = xmp.tile([P, PACK, CHUNK], BF16, name="xm")
             nc.vector.tensor_tensor(out=xm[:], in0=raw[b][:, :, cols],
                                     in1=mbc[b][:, cols].unsqueeze(1).to_broadcast([P, PACK, CHUNK]), op=ALU.mult)
             for j in range(PACK):
                 nc.vector.bn_stats(out=st[b][:, j, s, :], in_=xm[:, j, :])
-            grouped = grp.tile([P, CHUNK, PACK], BF16, name="grouped", align_bytes=64)
-            nc.scalar.copy(out=grouped[:].rearrange("p (c i) j -> p c j i", i=4),
-                           in_=raw[b][:, :, cols].rearrange("p j (c i) -> p c j i", i=4))
-            nc.vector.quantize_mx(out=xc[b][:, cols].bitcast(FP8X4), scales=xs[b][:, cols],
-                                  in_=grouped[:].rearrange("p w j -> p (w j)"))
-            if s == NCH - 1:
-                front_finish(b)
 
-        def front_finish(b):
+        def regroup(f):
+            b, s = divmod(f, NCH)
+            cols = slice(s * CHUNK, (s + 1) * CHUNK)
+            grouped = grp.tile([P, CHUNK, PACK], BF16, name="grouped", align_bytes=64)
+            dst = grouped[:].rearrange("p (c i) j -> p c j i", i=4)
+            src = raw[b][:, :, cols].rearrange("p j (c i) -> p c j i", i=4)
+            if f in RGG:
+                nc.gpsimd.tensor_scalar(out=dst, in0=src, scalar1=1.0, scalar2=0.0, op0=ALU.mult, op1=ALU.add)
+            else:
+                nc.scalar.copy(out=dst, in_=src)
+            gr[f] = grouped
+
+        def quant(f):
+            b, s = divmod(f, NCH)
+            cols = slice(s * CHUNK, (s + 1) * CHUNK)
+            if s == 0:
+                xc[b] = cod.tile([P, T], U32, name="xc", align_bytes=64)
+                xs[b] = cod.tile([P, T], U8, name="xs", align_bytes=64)
+            nc.vector.quantize_mx(out=xc[b][:, cols].bitcast(FP8X4), scales=xs[b][:, cols],
+                                  in_=gr.pop(f)[:].rearrange("p w j -> p (w j)"))
+
+        def aggr(b):
             mv = per.tile([P, PACK, 2], F32, name="mv")
             for j in range(PACK):
                 nc.vector.bn_aggr(out=mv[:, j, :], in_=st[b][:, j].rearrange("p s k -> p (s k)"))
@@ -164,6 +189,10 @@ def tile_attentivestatspool_pa_t_kernel(tc, x, mask, w1, b1, g1, be1, out):
             msb = per.tile([P, 2, P, PACK], BF16, name="msb", align_bytes=64)
             nc.gpsimd.tensor_scalar(out=msb[:], in0=ms[:].unsqueeze(2).to_broadcast([P, 2, P, PACK]),
                                     scalar1=1.0, scalar2=0.0, op0=ALU.mult, op1=ALU.add)
+            fin[b] = msb
+
+        def quant_ms(b):
+            msb = fin.pop(b)
             mc = per.tile([P, 2 * P], U32, name="mc", align_bytes=64)
             msc = per.tile([P, 2 * P], U8, name="msc", align_bytes=64)
             nc.vector.quantize_mx(out=mc[:].bitcast(FP8X4), scales=msc[:],
@@ -174,14 +203,22 @@ def tile_attentivestatspool_pa_t_kernel(tc, x, mask, w1, b1, g1, be1, out):
                                     lhsT_scale=msc[:, gi * P:(gi + 1) * P],
                                     rhs=w1c[:, 1 + gi, :].bitcast(FP8X4), rhs_scale=w1s[:, 1 + gi, :],
                                     start=(gi == 0), stop=(gi == 1))
+            fin[b] = ps_vb
+
+        def vb_add(b):
             vb[b] = per.tile([P, H], F32, name="vb")
-            nc.vector.tensor_tensor(out=vb[b][:], in0=ps_vb[:], in1=b1bc[:], op=ALU.add)
+            nc.vector.tensor_tensor(out=vb[b][:], in0=fin.pop(b)[:], in1=b1bc[:], op=ALU.add)
 
-        live = {}
+        pss = {}
+        av = {}
+        sums = {}
+        nrm = {}
+        zhs = {}
+        pts = {}
 
-        def stage1(g):
+        def mx(g):
             b, s = divmod(g, NCH)
-            a = up.tile([P, TILES, H], F32, name="a")
+            pss[g] = []
             for pair in range(TILES // 2):
                 ps = ps_mx.tile([P, 2, H], F32, name="ps")
                 for i in range(2):
@@ -190,55 +227,139 @@ def tile_attentivestatspool_pa_t_kernel(tc, x, mask, w1, b1, g1, be1, out):
                                         lhsT_scale=xs[b][:, t0:t0 + P],
                                         rhs=w1c[:, 0, :].bitcast(FP8X4), rhs_scale=w1s[:, 0, :],
                                         start=True, stop=True)
-                nc.vector.tensor_tensor(out=a[:, 2 * pair:2 * pair + 2, :], in0=ps[:],
+                pss[g].append(ps)
+
+        def p1(g):
+            b = g // NCH
+            a = up.tile([P, TILES, H], F32, name="a")
+            for pair in range(TILES // 2):
+                nc.vector.tensor_tensor(out=a[:, 2 * pair:2 * pair + 2, :], in0=pss[g][pair][:],
                                         in1=vb[b][:].unsqueeze(1).to_broadcast([P, 2, H]), op=ALU.add)
+            pss.pop(g)
+            av[g] = a
+
+        def relu(g):
+            a = av[g]
             s1 = sml.tile([P, TILES], F32, name="s1")
-            s2 = sml.tile([P, TILES], F32, name="s2")
             for k in range(TILES):
                 nc.scalar.activation(out=a[:, k, :], in_=a[:, k, :], func=ACT.Relu, accum_out=s1[:, k:k + 1])
-            for k in range(TILES):
-                junk = zp.tile([P, H], F32, name="junk")
-                nc.scalar.activation(out=junk[:], in_=a[:, k, :], func=ACT.Square, accum_out=s2[:, k:k + 1])
-            negmu = sml.tile([P, TILES], F32, name="negmu")
-            msq = sml.tile([P, TILES], F32, name="msq")
-            rstd = sml.tile([P, TILES], F32, name="rstd")
-            nc.gpsimd.tensor_scalar(out=negmu[:], in0=s1[:], scalar1=-1.0 / H, scalar2=0.0, op0=ALU.mult, op1=ALU.add)
-            nc.gpsimd.tensor_tensor(out=msq[:], in0=negmu[:], in1=negmu[:], op=ALU.mult)
-            nc.gpsimd.tensor_scalar(out=s2[:], in0=s2[:], scalar1=1.0 / H, scalar2=0.0, op0=ALU.mult, op1=ALU.add)
-            nc.gpsimd.tensor_tensor(out=msq[:], in0=s2[:], in1=msq[:], op=ALU.subtract)
-            nc.gpsimd.tensor_scalar(out=msq[:], in0=msq[:], scalar1=0.0, scalar2=EPS_LN, op0=ALU.max, op1=ALU.add)
-            nc.gpsimd.tensor_tensor(out=rstd[:], in0=msq[:], in1=nhalf[:], op=ALU.pow)
-            live[g] = (a, negmu, rstd)
+            sums[g] = s1
 
-        def stage2(g):
-            b, s = divmod(g, NCH)
-            a, negmu, rstd = live.pop(g)
+        def negmean(g):
+            negmu = sml.tile([P, TILES], F32, name="negmu")
+            nc.scalar.activation(out=negmu[:], in_=sums.pop(g)[:], func=ACT.Copy, scale=-1.0 / H)
+            nrm[g] = negmu
+
+        def sq_s(g):
+            a = av[g]
+            ns = TILES - NSQV[g]
+            if ns > 0:
+                s2s = sml.tile([P, TILES], F32, name="s2s")
+                for k in range(ns):
+                    junk = zp.tile([P, H], F32, name="junk")
+                    nc.scalar.activation(out=junk[:], in_=a[:, k, :], func=ACT.Square, bias=nrm[g][:, k:k + 1],
+                                         accum_out=s2s[:, k:k + 1])
+                sums[(g, 0)] = s2s
+
+        def sq_v(g):
+            a = av[g]
+            ns = TILES - NSQV[g]
+            s2v = sml.tile([P, TILES], F32, name="s2v")
+            for k in range(ns, TILES):
+                junkv = zp.tile([P, H], F32, name="junkv")
+                nc.vector.scalar_tensor_tensor(out=junkv[:], in0=a[:, k, :], scalar=nrm[g][:, k:k + 1], in1=a[:, k, :],
+                                               op0=ALU.add, op1=ALU.mult, accum_out=s2v[:, k:k + 1])
+            sums[(g, 1)] = s2v
+
+        def chain(g):
+            ns = TILES - NSQV[g]
+            ve = sml.tile([P, TILES], F32, name="ve")
+            rstd = sml.tile([P, TILES], F32, name="rstd")
+            if ns > 0:
+                nc.gpsimd.tensor_scalar(out=ve[:, 0:ns], in0=sums.pop((g, 0))[:, 0:ns], scalar1=1.0 / H, scalar2=EPS_LN,
+                                        op0=ALU.mult, op1=ALU.add)
+            if ns < TILES:
+                nc.gpsimd.tensor_scalar(out=ve[:, ns:TILES], in0=sums.pop((g, 1))[:, ns:TILES], scalar1=1.0 / H,
+                                        scalar2=EPS_LN, op0=ALU.mult, op1=ALU.add)
+                nc.gpsimd.tensor_scalar(out=ve[:, ns:TILES], in0=ve[:, ns:TILES], scalar1=EPS_LN, scalar2=None,
+                                        op0=ALU.max)
+            nc.gpsimd.tensor_tensor(out=rstd[:], in0=ve[:], in1=nhalf[:], op=ALU.pow)
+            nrm[g] = (nrm[g], rstd)
+
+        def p4(g):
+            a = av.pop(g)
+            negmu, rstd = nrm.pop(g)
             zh = zp.tile([P, TILES, H], F32, name="zh")
             for k in range(TILES):
-                nc.vector.tensor_scalar(out=zh[:, k, :], in0=a[:, k, :], scalar1=negmu[:, k:k + 1],
-                                        scalar2=rstd[:, k:k + 1], op0=ALU.add, op1=ALU.mult)
-            o = op.tile([P, 2, CHUNK], F32, name="o")
+                eng = nc.gpsimd if k < P4G[g] else nc.vector
+                eng.tensor_scalar(out=zh[:, k, :], in0=a[:, k, :], scalar1=negmu[:, k:k + 1],
+                                  scalar2=rstd[:, k:k + 1], op0=ALU.add, op1=ALU.mult)
+            zhs[g] = zh
+
+        def tr(g):
+            zh = zhs.pop(g)
+            pts[g] = []
             for hh in range(2):
                 pt = ps_tr.tile([P, CHUNK], F32, tag="tr", name="pt")
                 for k in range(TILES):
                     nc.tensor.transpose(out=pt[:, k * P:(k + 1) * P], in_=zh[:, k, hh * P:(hh + 1) * P],
                                         identity=ident_f[:])
-                nc.scalar.activation(out=o[:, hh, :], in_=pt[:], func=ACT.Tanh,
+                pts[g].append(pt)
+
+        def tanh_store(g):
+            b, s = divmod(g, NCH)
+            o = op.tile([P, 2, CHUNK], F32, name="o")
+            for hh in range(2):
+                nc.scalar.activation(out=o[:, hh, :], in_=pts[g][hh][:], func=ACT.Tanh,
                                      scale=gb[:, hh:hh + 1], bias=gb[:, 2 + hh:3 + hh])
+            pts.pop(g)
             nc.sync.dma_start(out=out[b].rearrange("(hh p) t -> p hh t", p=P)[:, :, s * CHUNK:(s + 1) * CHUNK],
                               in_=o[:])
 
-        n_f = B * NCH
-        front_chunk(0)
-        front_chunk(1)
-        totals_and_params()
-        w1_prep()
-        for f in range(2, LEAD):
-            front_chunk(f)
-        for g in range(n_f):
-            if g + LEAD < n_f:
-                front_chunk(g + LEAD)
-            stage1(g)
-            if g >= 1:
-                stage2(g - 1)
-        stage2(n_f - 1)
+        def ok(g):
+            return 0 <= g < NG
+
+        P4O = 3
+        THO = P4O + 1
+        for i in range(-LEAD, NG + THO + 1):
+            f = i + LEAD
+            if ok(i + 1):
+                mx(i + 1)
+            if ok(i):
+                p1(i)
+            if ok(i - 1):
+                relu(i - 1)
+            if ok(i - THO):
+                tanh_store(i - THO)
+            if ok(i - 1):
+                negmean(i - 1)
+                sq_s(i - 1)
+                if NSQV[i - 1] == 0:
+                    chain(i - 1)
+            if ok(i - 2) and NSQV[i - 2] > 0:
+                sq_v(i - 2)
+                chain(i - 2)
+            if ok(i - P4O):
+                p4(i - P4O)
+                tr(i - P4O)
+            if ok(f):
+                tt_bn(f)
+            if f == 2:
+                totals()
+            if f == 3:
+                params()
+                w1_quant()
+            if ok(f - 1):
+                quant(f - 1)
+            if ok(f) and f % NCH == NCH - 1:
+                aggr(f // NCH)
+            if ok(f - 1) and (f - 1) % NCH == NCH - 1:
+                quant_ms((f - 1) // NCH)
+            if ok(f - 2) and (f - 2) % NCH == NCH - 1:
+                vb_add((f - 2) // NCH)
+            if ok(f):
+                regroup(f)
+            if f == 1:
+                w1_permute()
+            if f == 2:
+                w1_transpose()

@@ -19,13 +19,13 @@ CHUNK = 512
 NCH = T // CHUNK
 TILES = CHUNK // P
 NG = B * NCH
+NQ = T // P
 EPS_LN = 1e-5
 EPS_STD = 1e-5
 LEAD = 6
-PINNED = True
-NSQV = [0,0,0,0,0,0,0,0,0,0,0,0,4,4,4,4]
-P4G = [0,0,0,0,0,0,0,0,0,0,0,0,0,0,0,0]
-RGG = []
+P4O = 3
+BCS_AT = 2
+VSQ = [12,13,14,15]
 FLOPS = 2 * B * H * 3 * C * T
 
 
@@ -41,37 +41,27 @@ def tile_attentivestatspool_pa_t_kernel(tc, x, mask, w1, b1, g1, be1, out):
         up = ctx.enter_context(tc.tile_pool(name="up", bufs=6))
         zp = ctx.enter_context(tc.tile_pool(name="zp", bufs=3))
         op = ctx.enter_context(tc.tile_pool(name="op", bufs=3))
-        ps_mx = ctx.enter_context(tc.psum_pool(name="ps_mx", bufs=4))
+        ps_mx = ctx.enter_context(tc.psum_pool(name="ps_mx", bufs=3))
         ps_tr = ctx.enter_context(tc.psum_pool(name="ps_tr", bufs=3))
         ps_ms = ctx.enter_context(tc.psum_pool(name="ps_ms", bufs=1))
-        if PINNED:
-            ctx.enter_context(tc.manual_schedule())
+        ps_mk = ctx.enter_context(tc.psum_pool(name="ps_mk", bufs=1))
+        ctx.enter_context(tc.manual_schedule())
 
-        raw = []
-        mbc = []
-        for b in range(B):
-            raw.append(const.tile([P, PACK, T], BF16, name="raw%d" % b))
-            mbc.append(const.tile([P, T], BF16, name="mbc%d" % b))
-        msk = const.tile([P, T * B // P], BF16, name="msk")
+        raw = [const.tile([P, PACK, T], BF16, name="raw%d" % b) for b in range(B)]
         w1_sb = const.tile([P, 2, 3 * C], BF16, name="w1_sb")
-        b1bc = const.tile([P, H], BF16, name="b1bc")
         pr = const.tile([P, P], BF16, name="pr")
         nc.vector.memset(pr[:], 0.0)
-        mask_rows = mask.rearrange("b o t -> (b o) t")
         x_v = [x[b].rearrange("(p j) t -> p j t", j=PACK) for b in range(B)]
+        nc.scalar.dma_start(out=pr[0:B * NQ, :], in_=mask.rearrange("b o (q r) -> (b o q) r", r=P))
+        nc.scalar.dma_start(out=pr[64:66, :], in_=g1.rearrange("(r f) -> r f", f=P))
+        nc.scalar.dma_start(out=pr[66:68, :], in_=be1.rearrange("(r f) -> r f", f=P))
+        nc.scalar.dma_start(out=pr[68:70, :], in_=b1.rearrange("(r f) -> r f", f=P))
         for s in range(NCH):
             nc.sync.dma_start(out=raw[0][:, :, s * CHUNK:(s + 1) * CHUNK],
                               in_=x_v[0][:, :, s * CHUNK:(s + 1) * CHUNK])
         nc.sync.dma_start(out=w1_sb[:], in_=w1.rearrange("(hh p) k -> p hh k", p=P))
         for b in range(1, B):
             nc.sync.dma_start(out=raw[b][:], in_=x_v[b])
-        nc.scalar.dma_start(out=mbc[0][:], in_=mask_rows[0].partition_broadcast(P))
-        nc.scalar.dma_start(out=msk[:], in_=mask.rearrange("b o (r f) -> (b o r) f", f=T * B // P))
-        nc.scalar.dma_start(out=b1bc[:], in_=b1.partition_broadcast(P))
-        nc.scalar.dma_start(out=pr[0:2, :], in_=g1.rearrange("(r f) -> r f", f=P))
-        nc.scalar.dma_start(out=pr[2:4, :], in_=be1.rearrange("(r f) -> r f", f=P))
-        for b in range(1, B):
-            nc.scalar.dma_start(out=mbc[b][:], in_=mask_rows[b].partition_broadcast(P))
 
         ident_b = const.tile([P, P], BF16, name="ident_b")
         make_identity(nc, ident_b[:])
@@ -83,33 +73,37 @@ def tile_attentivestatspool_pa_t_kernel(tc, x, mask, w1, b1, g1, be1, out):
         nc.vector.memset(half[:], 0.5)
         nhalf = const.tile([P, TILES], F32, name="nhalf")
         nc.vector.memset(nhalf[:], -0.5)
-        ind = const.tile([P, 32], F32, name="ind")
-        nc.vector.memset(ind[:], 0.0)
+        rhs_tot = const.tile([P, 32], F32, name="rhs_tot")
+        nc.vector.memset(rhs_tot[:], 0.0)
 
         w1c = const.tile([P, 3, H], U32, name="w1c", align_bytes=64)
         w1s = const.tile([P, 3, H], U8, name="w1s", align_bytes=64)
         w1p = const.tile([P, 2, 3, PACK, P], BF16, name="w1p")
         w1g = const.tile([P, 3, H, PACK], BF16, name="w1g", align_bytes=64)
+        cols = const.tile([P, 72], BF16, name="cols")
         gb = const.tile([P, 4], F32, name="gb")
         r_t = const.tile([P, B], F32, name="r_t")
+        b1bc = const.tile([P, H], BF16, name="b1bc")
+
+        def columns():
+            ps_pr = ps_ms.tile([P, P], BF16, tag="ms", name="ps_pr")
+            nc.tensor.transpose(out=ps_pr[:], in_=pr[:], identity=ident_b[:])
+            nc.vector.tensor_copy(out=cols[:, 0:70], in_=ps_pr[:, 0:70])
+            nc.vector.tensor_copy(out=gb[:], in_=ps_pr[:, 64:68])
 
         def totals():
-            part = const.tile([P, 1], F32, name="part")
-            nc.vector.tensor_reduce(out=part[:], in_=msk[:], axis=AX.X, op=ALU.add)
-            nc.vector.tensor_reduce(out=ind[:, 0:B], in_=ident_f[:].rearrange("p (b q) -> p b q", b=B),
+            nc.vector.tensor_reduce(out=rhs_tot[:, 0:B], in_=cols[:, 0:B * NQ].rearrange("p (b q) -> p b q", b=B),
                                     axis=AX.X, op=ALU.add)
-            rhs_tot = const.tile([P, 32], F32, name="rhs_tot")
-            nc.vector.tensor_scalar(out=rhs_tot[:], in0=ind[:], scalar1=part[:, 0:1], scalar2=None, op0=ALU.mult)
             ps_tot = ps_ms.tile([P, 32], F32, tag="ms", name="ps_tot")
             nc.tensor.matmul(out=ps_tot[:], lhsT=ones_f[:], rhs=rhs_tot[:], start=True, stop=True)
             rtot = const.tile([P, B], F32, name="rtot")
             nc.vector.reciprocal(out=rtot[:], in_=ps_tot[:, 0:B])
             nc.vector.tensor_scalar(out=r_t[:], in0=rtot[:], scalar1=float(T), scalar2=None, op0=ALU.mult)
-
-        def params():
-            ps_pr = ps_ms.tile([P, P], BF16, tag="ms", name="ps_pr")
-            nc.tensor.transpose(out=ps_pr[:], in_=pr[:], identity=ident_b[:])
-            nc.vector.tensor_copy(out=gb[:], in_=ps_pr[:, 0:4])
+            ps_b1 = ps_ms.tile([P, H], BF16, tag="ms", name="ps_b1")
+            for hh in range(2):
+                nc.tensor.transpose(out=ps_b1[:, hh * P:(hh + 1) * P],
+                                    in_=cols[:, 68 + hh:69 + hh].to_broadcast([P, P]), identity=ident_b[:])
+            nc.vector.tensor_copy(out=b1bc[:], in_=ps_b1[:])
 
         def w1_permute():
             for hh in range(2):
@@ -134,80 +128,98 @@ def tile_attentivestatspool_pa_t_kernel(tc, x, mask, w1, b1, g1, be1, out):
         st = {}
         vb = {}
         gr = {}
+        mk = {}
         fin = {}
 
-        def tt_bn(f):
+        def mask_bc(f):
             b, s = divmod(f, NCH)
-            cols = slice(s * CHUNK, (s + 1) * CHUNK)
+            pmk = ps_mk.tile([P, CHUNK], BF16, name="pmk")
+            for k in range(TILES):
+                c = b * NQ + s * TILES + k
+                nc.tensor.transpose(out=pmk[:, k * P:(k + 1) * P], in_=cols[:, c:c + 1].to_broadcast([P, P]),
+                                    identity=ident_b[:])
+            mk[f] = pmk
+
+        def tt_bn(f, between):
+            b, s = divmod(f, NCH)
+            cols_f = slice(s * CHUNK, (s + 1) * CHUNK)
             if s == 0:
                 st[b] = per.tile([P, PACK, NCH, 6], F32, name="st")
             xm = xmp.tile([P, PACK, CHUNK], BF16, name="xm")
-            nc.vector.tensor_tensor(out=xm[:], in0=raw[b][:, :, cols],
-                                    in1=mbc[b][:, cols].unsqueeze(1).to_broadcast([P, PACK, CHUNK]), op=ALU.mult)
+            nc.vector.tensor_tensor(out=xm[:], in0=raw[b][:, :, cols_f],
+                                    in1=mk.pop(f)[:].unsqueeze(1).to_broadcast([P, PACK, CHUNK]), op=ALU.mult)
+            if f + 1 < NG:
+                mask_bc(f + 1)
             for j in range(PACK):
+                if j < len(between):
+                    between[j]()
                 nc.vector.bn_stats(out=st[b][:, j, s, :], in_=xm[:, j, :])
 
         def regroup(f):
             b, s = divmod(f, NCH)
-            cols = slice(s * CHUNK, (s + 1) * CHUNK)
+            cols_f = slice(s * CHUNK, (s + 1) * CHUNK)
             grouped = grp.tile([P, CHUNK, PACK], BF16, name="grouped", align_bytes=64)
-            dst = grouped[:].rearrange("p (c i) j -> p c j i", i=4)
-            src = raw[b][:, :, cols].rearrange("p j (c i) -> p c j i", i=4)
-            if f in RGG:
-                nc.gpsimd.tensor_scalar(out=dst, in0=src, scalar1=1.0, scalar2=0.0, op0=ALU.mult, op1=ALU.add)
-            else:
-                nc.scalar.copy(out=dst, in_=src)
+            nc.scalar.copy(out=grouped[:].rearrange("p (c i) j -> p c j i", i=4),
+                           in_=raw[b][:, :, cols_f].rearrange("p j (c i) -> p c j i", i=4))
             gr[f] = grouped
 
         def quant(f):
             b, s = divmod(f, NCH)
-            cols = slice(s * CHUNK, (s + 1) * CHUNK)
+            cols_f = slice(s * CHUNK, (s + 1) * CHUNK)
             if s == 0:
                 xc[b] = cod.tile([P, T], U32, name="xc", align_bytes=64)
                 xs[b] = cod.tile([P, T], U8, name="xs", align_bytes=64)
-            nc.vector.quantize_mx(out=xc[b][:, cols].bitcast(FP8X4), scales=xs[b][:, cols],
+            nc.vector.quantize_mx(out=xc[b][:, cols_f].bitcast(FP8X4), scales=xs[b][:, cols_f],
                                   in_=gr.pop(f)[:].rearrange("p w j -> p (w j)"))
 
         def aggr(b):
             mv = per.tile([P, PACK, 2], F32, name="mv")
             for j in range(PACK):
                 nc.vector.bn_aggr(out=mv[:, j, :], in_=st[b][:, j].rearrange("p s k -> p (s k)"))
-            mean = mv[:, :, 0]
-            var = mv[:, :, 1]
-            rb = r_t[:, b:b + 1]
-            ms = per.tile([P, 2, PACK], F32, name="ms")
-            d = per.tile([P, PACK], F32, name="d")
-            t1 = per.tile([P, PACK], F32, name="t1")
-            vr = per.tile([P, PACK], F32, name="vr")
-            nc.gpsimd.tensor_scalar(out=ms[:, 0, :], in0=mean, scalar1=rb, scalar2=0.0, op0=ALU.mult, op1=ALU.add)
-            nc.gpsimd.tensor_tensor(out=d[:], in0=mean, in1=ms[:, 0, :], op=ALU.subtract)
-            nc.gpsimd.tensor_tensor(out=t1[:], in0=ms[:, 0, :], in1=d[:], op=ALU.mult)
-            nc.gpsimd.tensor_scalar(out=vr[:], in0=var, scalar1=rb, scalar2=0.0, op0=ALU.mult, op1=ALU.add)
-            nc.gpsimd.tensor_tensor(out=vr[:], in0=vr[:], in1=t1[:], op=ALU.add)
-            nc.gpsimd.tensor_scalar(out=vr[:], in0=vr[:], scalar1=EPS_STD, scalar2=None, op0=ALU.max)
-            nc.gpsimd.tensor_tensor(out=ms[:, 1, :], in0=vr[:], in1=half[:], op=ALU.pow)
-            msb = per.tile([P, 2, P, PACK], BF16, name="msb", align_bytes=64)
-            nc.gpsimd.tensor_scalar(out=msb[:], in0=ms[:].unsqueeze(2).to_broadcast([P, 2, P, PACK]),
-                                    scalar1=1.0, scalar2=0.0, op0=ALU.mult, op1=ALU.add)
-            fin[b] = msb
+            fin[b] = {"mv": mv}
 
-        def quant_ms(b):
-            msb = fin.pop(b)
-            mc = per.tile([P, 2 * P], U32, name="mc", align_bytes=64)
-            msc = per.tile([P, 2 * P], U8, name="msc", align_bytes=64)
-            nc.vector.quantize_mx(out=mc[:].bitcast(FP8X4), scales=msc[:],
-                                  in_=msb[:].rearrange("p g w j -> p (g w j)"))
-            ps_vb = ps_ms.tile([P, H], F32, tag="ms", name="ps_vb")
-            for gi in range(2):
-                nc.tensor.matmul_mx(out=ps_vb[:], lhsT=mc[:, gi * P:(gi + 1) * P].bitcast(FP8X4),
-                                    lhsT_scale=msc[:, gi * P:(gi + 1) * P],
-                                    rhs=w1c[:, 1 + gi, :].bitcast(FP8X4), rhs_scale=w1s[:, 1 + gi, :],
-                                    start=(gi == 0), stop=(gi == 1))
-            fin[b] = ps_vb
+        def stat_ops(b):
+            e = fin[b]
+            mean = e["mv"][:, :, 0]
+            var = e["mv"][:, :, 1]
+            rb = r_t[:, b:b + 1]
+            m0 = per.tile([P, PACK], F32, name="m0")
+            d = per.tile([P, PACK], F32, name="d")
+            v0 = per.tile([P, PACK], F32, name="v0")
+            e["m0"] = m0
+            e["v0"] = v0
+            return [
+                lambda: nc.vector.tensor_scalar(out=m0[:], in0=mean, scalar1=rb, scalar2=None, op0=ALU.mult),
+                lambda: nc.vector.tensor_tensor(out=d[:], in0=mean, in1=m0[:], op=ALU.subtract),
+                lambda: nc.vector.tensor_tensor(out=d[:], in0=m0[:], in1=d[:], op=ALU.mult),
+                lambda: nc.vector.scalar_tensor_tensor(out=v0[:], in0=var, scalar=rb, in1=d[:],
+                                                       op0=ALU.mult, op1=ALU.add),
+            ]
+
+        def spread(b, gi, src):
+            e = fin[b]
+            msb = per.tile([P, P, PACK], BF16, name="msb%d" % gi, align_bytes=64)
+            nc.vector.tensor_copy(out=msb[:], in_=src[:].unsqueeze(1).to_broadcast([P, P, PACK]))
+            mc = per.tile([P, P], U32, name="mc%d" % gi, align_bytes=64)
+            msc = per.tile([P, P], U8, name="msc%d" % gi, align_bytes=64)
+            nc.vector.quantize_mx(out=mc[:].bitcast(FP8X4), scales=msc[:], in_=msb[:].rearrange("p w j -> p (w j)"))
+            if gi == 0:
+                e["ps"] = ps_ms.tile([P, H], F32, tag="ms", name="ps_vb")
+            nc.tensor.matmul_mx(out=e["ps"][:], lhsT=mc[:].bitcast(FP8X4), lhsT_scale=msc[:],
+                                rhs=w1c[:, 1 + gi, :].bitcast(FP8X4), rhs_scale=w1s[:, 1 + gi, :],
+                                start=(gi == 0), stop=(gi == 1))
+
+        def stat_tail(b):
+            e = fin[b]
+            nc.vector.tensor_scalar(out=e["v0"][:], in0=e["v0"][:], scalar1=EPS_STD, scalar2=None, op0=ALU.max)
+            std = per.tile([P, PACK], F32, name="std")
+            nc.gpsimd.tensor_tensor(out=std[:], in0=e["v0"][:], in1=half[:], op=ALU.pow)
+            e["std"] = std
+            spread(b, 0, e["m0"])
 
         def vb_add(b):
             vb[b] = per.tile([P, H], F32, name="vb")
-            nc.vector.tensor_tensor(out=vb[b][:], in0=fin.pop(b)[:], in1=b1bc[:], op=ALU.add)
+            nc.vector.tensor_tensor(out=vb[b][:], in0=fin.pop(b)["ps"][:], in1=b1bc[:], op=ALU.add)
 
         pss = {}
         av = {}
@@ -237,6 +249,13 @@ def tile_attentivestatspool_pa_t_kernel(tc, x, mask, w1, b1, g1, be1, out):
                                         in1=vb[b][:].unsqueeze(1).to_broadcast([P, 2, H]), op=ALU.add)
             pss.pop(g)
             av[g] = a
+            if g in VSQ:
+                s2v = sml.tile([P, TILES], F32, name="s2v")
+                for k in range(TILES):
+                    junkv = zp.tile([P, H], F32, name="junkv")
+                    nc.vector.scalar_tensor_tensor(out=junkv[:], in0=a[:, k, :], scalar=0.0, in1=a[:, k, :],
+                                                   op0=ALU.max, op1=ALU.mult, accum_out=s2v[:, k:k + 1])
+                sums[(g, 1)] = s2v
 
         def relu(g):
             a = av[g]
@@ -245,44 +264,33 @@ def tile_attentivestatspool_pa_t_kernel(tc, x, mask, w1, b1, g1, be1, out):
                 nc.scalar.activation(out=a[:, k, :], in_=a[:, k, :], func=ACT.Relu, accum_out=s1[:, k:k + 1])
             sums[g] = s1
 
-        def negmean(g):
+        def variance_s(g):
+            a = av[g]
             negmu = sml.tile([P, TILES], F32, name="negmu")
             nc.scalar.activation(out=negmu[:], in_=sums.pop(g)[:], func=ACT.Copy, scale=-1.0 / H)
             nrm[g] = negmu
-
-        def sq_s(g):
-            a = av[g]
-            ns = TILES - NSQV[g]
-            if ns > 0:
+            if g not in VSQ:
                 s2s = sml.tile([P, TILES], F32, name="s2s")
-                for k in range(ns):
+                for k in range(TILES):
                     junk = zp.tile([P, H], F32, name="junk")
-                    nc.scalar.activation(out=junk[:], in_=a[:, k, :], func=ACT.Square, bias=nrm[g][:, k:k + 1],
+                    nc.scalar.activation(out=junk[:], in_=a[:, k, :], func=ACT.Square, bias=negmu[:, k:k + 1],
                                          accum_out=s2s[:, k:k + 1])
-                sums[(g, 0)] = s2s
+                ve = sml.tile([P, TILES], F32, name="ve")
+                nc.scalar.activation(out=ve[:], in_=s2s[:], func=ACT.Copy, scale=1.0 / H, bias=EPS_LN)
+                rsqrt(g, ve)
 
-        def sq_v(g):
-            a = av[g]
-            ns = TILES - NSQV[g]
-            s2v = sml.tile([P, TILES], F32, name="s2v")
-            for k in range(ns, TILES):
-                junkv = zp.tile([P, H], F32, name="junkv")
-                nc.vector.scalar_tensor_tensor(out=junkv[:], in0=a[:, k, :], scalar=nrm[g][:, k:k + 1], in1=a[:, k, :],
-                                               op0=ALU.add, op1=ALU.mult, accum_out=s2v[:, k:k + 1])
-            sums[(g, 1)] = s2v
+        def variance_v(g):
+            negmu = nrm[g]
+            msq = sml.tile([P, TILES], F32, name="msq")
+            vev = sml.tile([P, TILES], F32, name="vev")
+            nc.vector.tensor_tensor(out=msq[:], in0=negmu[:], in1=negmu[:], op=ALU.mult)
+            nc.vector.scalar_tensor_tensor(out=vev[:], in0=sums.pop((g, 1))[:], scalar=1.0 / H, in1=msq[:],
+                                           op0=ALU.mult, op1=ALU.subtract)
+            nc.vector.tensor_scalar(out=vev[:], in0=vev[:], scalar1=0.0, scalar2=EPS_LN, op0=ALU.max, op1=ALU.add)
+            rsqrt(g, vev)
 
-        def chain(g):
-            ns = TILES - NSQV[g]
-            ve = sml.tile([P, TILES], F32, name="ve")
+        def rsqrt(g, ve):
             rstd = sml.tile([P, TILES], F32, name="rstd")
-            if ns > 0:
-                nc.gpsimd.tensor_scalar(out=ve[:, 0:ns], in0=sums.pop((g, 0))[:, 0:ns], scalar1=1.0 / H, scalar2=EPS_LN,
-                                        op0=ALU.mult, op1=ALU.add)
-            if ns < TILES:
-                nc.gpsimd.tensor_scalar(out=ve[:, ns:TILES], in0=sums.pop((g, 1))[:, ns:TILES], scalar1=1.0 / H,
-                                        scalar2=EPS_LN, op0=ALU.mult, op1=ALU.add)
-                nc.gpsimd.tensor_scalar(out=ve[:, ns:TILES], in0=ve[:, ns:TILES], scalar1=EPS_LN, scalar2=None,
-                                        op0=ALU.max)
             nc.gpsimd.tensor_tensor(out=rstd[:], in0=ve[:], in1=nhalf[:], op=ALU.pow)
             nrm[g] = (nrm[g], rstd)
 
@@ -291,13 +299,8 @@ def tile_attentivestatspool_pa_t_kernel(tc, x, mask, w1, b1, g1, be1, out):
             negmu, rstd = nrm.pop(g)
             zh = zp.tile([P, TILES, H], F32, name="zh")
             for k in range(TILES):
-                eng = nc.gpsimd if k < P4G[g] else nc.vector
-                eng.tensor_scalar(out=zh[:, k, :], in0=a[:, k, :], scalar1=negmu[:, k:k + 1],
-                                  scalar2=rstd[:, k:k + 1], op0=ALU.add, op1=ALU.mult)
-            zhs[g] = zh
-
-        def tr(g):
-            zh = zhs.pop(g)
+                nc.vector.tensor_scalar(out=zh[:, k, :], in0=a[:, k, :], scalar1=negmu[:, k:k + 1],
+                                        scalar2=rstd[:, k:k + 1], op0=ALU.add, op1=ALU.mult)
             pts[g] = []
             for hh in range(2):
                 pt = ps_tr.tile([P, CHUNK], F32, tag="tr", name="pt")
@@ -319,47 +322,50 @@ def tile_attentivestatspool_pa_t_kernel(tc, x, mask, w1, b1, g1, be1, out):
         def ok(g):
             return 0 <= g < NG
 
-        P4O = 3
-        THO = P4O + 1
-        for i in range(-LEAD, NG + THO + 1):
+        def closed(f, k):
+            return (f - k) // NCH if ok(f - k) and (f - k) % NCH == NCH - 1 else -1
+
+        columns()
+        mask_bc(0)
+        for i in range(-LEAD, NG + P4O + 2):
             f = i + LEAD
+            b_1 = closed(f, 1)
+            between = stat_ops(b_1) if b_1 >= 0 else []
+            if ok(f):
+                tt_bn(f, between)
+            else:
+                for fn in between:
+                    fn()
+            if b_1 >= 0:
+                stat_tail(b_1)
+            if f == 1:
+                totals()
+            if closed(f, 0) >= 0:
+                aggr(closed(f, 0))
             if ok(i + 1):
                 mx(i + 1)
+            if closed(f, BCS_AT + 1) >= 0:
+                vb_add(closed(f, BCS_AT + 1))
             if ok(i):
                 p1(i)
-            if ok(i - 1):
-                relu(i - 1)
-            if ok(i - THO):
-                tanh_store(i - THO)
-            if ok(i - 1):
-                negmean(i - 1)
-                sq_s(i - 1)
-                if NSQV[i - 1] == 0:
-                    chain(i - 1)
-            if ok(i - 2) and NSQV[i - 2] > 0:
-                sq_v(i - 2)
-                chain(i - 2)
+            if ok(i - 2) and (i - 2) in VSQ:
+                variance_v(i - 2)
             if ok(i - P4O):
                 p4(i - P4O)
-                tr(i - P4O)
-            if ok(f):
-                tt_bn(f)
-            if f == 2:
-                totals()
             if f == 3:
-                params()
                 w1_quant()
             if ok(f - 1):
                 quant(f - 1)
-            if ok(f) and f % NCH == NCH - 1:
-                aggr(f // NCH)
-            if ok(f - 1) and (f - 1) % NCH == NCH - 1:
-                quant_ms((f - 1) // NCH)
-            if ok(f - 2) and (f - 2) % NCH == NCH - 1:
-                vb_add((f - 2) // NCH)
+            if closed(f, BCS_AT) >= 0:
+                spread(closed(f, BCS_AT), 1, fin[closed(f, BCS_AT)]["std"])
+            if ok(i - 1):
+                relu(i - 1)
+                variance_s(i - 1)
             if ok(f):
                 regroup(f)
             if f == 1:
                 w1_permute()
             if f == 2:
                 w1_transpose()
+            if ok(i - P4O - 1):
+                tanh_store(i - P4O - 1)

@@ -22,10 +22,12 @@ NG = B * NCH
 NQ = T // P
 EPS_LN = 1e-5
 EPS_STD = 1e-5
-LEAD = 6
-P4O = 3
-BCS_AT = 2
-VSQ = [12,13,14,15]
+LEAD = 5
+P4O = 2
+RGA = 3
+P4V_FROM = 12
+BCS_AT = 1
+VSQ = [14,15]
 FLOPS = 2 * B * H * 3 * C * T
 
 
@@ -34,11 +36,11 @@ def tile_attentivestatspool_pa_t_kernel(tc, x, mask, w1, b1, g1, be1, out):
     with ExitStack() as ctx:
         const = ctx.enter_context(tc.tile_pool(name="const", bufs=1))
         xmp = ctx.enter_context(tc.tile_pool(name="xmp", bufs=3))
-        grp = ctx.enter_context(tc.tile_pool(name="grp", bufs=3))
+        grp = ctx.enter_context(tc.tile_pool(name="grp", bufs=6))
         cod = ctx.enter_context(tc.tile_pool(name="cod", bufs=3))
         sml = ctx.enter_context(tc.tile_pool(name="sml", bufs=6))
         per = ctx.enter_context(tc.tile_pool(name="per", bufs=2))
-        up = ctx.enter_context(tc.tile_pool(name="up", bufs=6))
+        up = ctx.enter_context(tc.tile_pool(name="up", bufs=5))
         zp = ctx.enter_context(tc.tile_pool(name="zp", bufs=3))
         op = ctx.enter_context(tc.tile_pool(name="op", bufs=3))
         ps_mx = ctx.enter_context(tc.psum_pool(name="ps_mx", bufs=3))
@@ -293,14 +295,20 @@ def tile_attentivestatspool_pa_t_kernel(tc, x, mask, w1, b1, g1, be1, out):
             rstd = sml.tile([P, TILES], F32, name="rstd")
             nc.gpsimd.tensor_tensor(out=rstd[:], in0=ve[:], in1=nhalf[:], op=ALU.pow)
             nrm[g] = (nrm[g], rstd)
+            if g < P4V_FROM:
+                normalise(g, nc.gpsimd)
 
-        def p4(g):
+        def normalise(g, eng):
             a = av.pop(g)
             negmu, rstd = nrm.pop(g)
             zh = zp.tile([P, TILES, H], F32, name="zh")
             for k in range(TILES):
-                nc.vector.tensor_scalar(out=zh[:, k, :], in0=a[:, k, :], scalar1=negmu[:, k:k + 1],
-                                        scalar2=rstd[:, k:k + 1], op0=ALU.add, op1=ALU.mult)
+                eng.tensor_scalar(out=zh[:, k, :], in0=a[:, k, :], scalar1=negmu[:, k:k + 1],
+                                  scalar2=rstd[:, k:k + 1], op0=ALU.add, op1=ALU.mult)
+            zhs[g] = zh
+
+        def p4(g):
+            zh = zhs.pop(g)
             pts[g] = []
             for hh in range(2):
                 pt = ps_tr.tile([P, CHUNK], F32, tag="tr", name="pt")
@@ -327,6 +335,8 @@ def tile_attentivestatspool_pa_t_kernel(tc, x, mask, w1, b1, g1, be1, out):
 
         columns()
         mask_bc(0)
+        done = {"rg": 0, "q": 0}
+        rg_step = {}
         for i in range(-LEAD, NG + P4O + 2):
             f = i + LEAD
             b_1 = closed(f, 1)
@@ -350,22 +360,27 @@ def tile_attentivestatspool_pa_t_kernel(tc, x, mask, w1, b1, g1, be1, out):
                 p1(i)
             if ok(i - 2) and (i - 2) in VSQ:
                 variance_v(i - 2)
-            if ok(i - P4O):
-                p4(i - P4O)
+            if ok(i - 2) and i - 2 >= P4V_FROM:
+                normalise(i - 2, nc.vector)
             if f == 3:
                 w1_quant()
-            if ok(f - 1):
-                quant(f - 1)
+            while done["q"] < done["rg"] and rg_step[done["q"]] < i:
+                quant(done["q"])
+                done["q"] = done["q"] + 1
             if closed(f, BCS_AT) >= 0:
                 spread(closed(f, BCS_AT), 1, fin[closed(f, BCS_AT)]["std"])
             if ok(i - 1):
                 relu(i - 1)
                 variance_s(i - 1)
-            if ok(f):
-                regroup(f)
+            if ok(i - P4O):
+                p4(i - P4O)
             if f == 1:
                 w1_permute()
             if f == 2:
                 w1_transpose()
+            while done["rg"] <= min(NG - 1, f + RGA):
+                regroup(done["rg"])
+                rg_step[done["rg"]] = i
+                done["rg"] = done["rg"] + 1
             if ok(i - P4O - 1):
                 tanh_store(i - P4O - 1)

@@ -201,7 +201,16 @@ def tile_attentivestatspool_pa_t_kernel(tc, x, mask, w1, b1, g1, be1, out):
         def spread(b, gi, src):
             e = fin[b]
             msb = per.tile([P, P, PACK], BF16, name="msb%d" % gi, align_bytes=64)
-            nc.vector.tensor_copy(out=msb[:], in_=src[:].unsqueeze(1).to_broadcast([P, P, PACK]))
+            if b < B - 1:
+                nc.gpsimd.tensor_scalar(out=msb[:], in0=src[:].unsqueeze(1).to_broadcast([P, P, PACK]),
+                                        scalar1=1.0, scalar2=0.0, op0=ALU.mult, op1=ALU.add)
+            else:
+                nc.vector.tensor_copy(out=msb[:], in_=src[:].unsqueeze(1).to_broadcast([P, P, PACK]))
+            e["msb%d" % gi] = msb
+
+        def spread_q(b, gi):
+            e = fin[b]
+            msb = e["msb%d" % gi]
             mc = per.tile([P, P], U32, name="mc%d" % gi, align_bytes=64)
             msc = per.tile([P, P], U8, name="msc%d" % gi, align_bytes=64)
             nc.vector.quantize_mx(out=mc[:].bitcast(FP8X4), scales=msc[:], in_=msb[:].rearrange("p w j -> p (w j)"))
@@ -218,6 +227,10 @@ def tile_attentivestatspool_pa_t_kernel(tc, x, mask, w1, b1, g1, be1, out):
             nc.gpsimd.tensor_tensor(out=std[:], in0=e["v0"][:], in1=half[:], op=ALU.pow)
             e["std"] = std
             spread(b, 0, e["m0"])
+            if b < B - 1:
+                spread(b, 1, std)
+            else:
+                spread_q(b, 0)
 
         def vb_add(b):
             vb[b] = per.tile([P, H], F32, name="vb")
@@ -341,6 +354,9 @@ def tile_attentivestatspool_pa_t_kernel(tc, x, mask, w1, b1, g1, be1, out):
             f = i + LEAD
             b_1 = closed(f, 1)
             between = stat_ops(b_1) if b_1 >= 0 else []
+            if 0 <= closed(f, 2) < B - 1:
+                b_2 = closed(f, 2)
+                between = [lambda: None, lambda: None, lambda: spread_q(b_2, 0), lambda: spread_q(b_2, 1)]
             if ok(f):
                 tt_bn(f, between)
             else:
@@ -367,8 +383,9 @@ def tile_attentivestatspool_pa_t_kernel(tc, x, mask, w1, b1, g1, be1, out):
             while done["q"] < done["rg"] and rg_step[done["q"]] < i:
                 quant(done["q"])
                 done["q"] = done["q"] + 1
-            if closed(f, BCS_AT) >= 0:
-                spread(closed(f, BCS_AT), 1, fin[closed(f, BCS_AT)]["std"])
+            if b_1 == B - 1:
+                spread(b_1, 1, fin[b_1]["std"])
+                spread_q(b_1, 1)
             if ok(i - 1):
                 relu(i - 1)
                 variance_s(i - 1)

@@ -336,9 +336,12 @@ def tile_attentivestatspool_pa_t_kernel(tc, x, mask, w1, b1, g1, be1, out):
             for hh in range(2):
                 nc.scalar.activation(out=o[:, hh, :], in_=pts[g][hh][:], func=ACT.Tanh,
                                      scale=gb[:, hh:hh + 1], bias=gb[:, 2 + hh:3 + hh])
+                if g == NG - 1:
+                    nc.sync.dma_start(out=out[b][hh * P:(hh + 1) * P, s * CHUNK:(s + 1) * CHUNK], in_=o[:, hh, :])
             pts.pop(g)
-            nc.sync.dma_start(out=out[b].rearrange("(hh p) t -> p hh t", p=P)[:, :, s * CHUNK:(s + 1) * CHUNK],
-                              in_=o[:])
+            if g < NG - 1:
+                nc.sync.dma_start(out=out[b].rearrange("(hh p) t -> p hh t", p=P)[:, :, s * CHUNK:(s + 1) * CHUNK],
+                                  in_=o[:])
 
         def ok(g):
             return 0 <= g < NG

from contextlib import ExitStack

import concourse.mybir as mybir
from concourse.masks import make_identity

F32 = mybir.dt.float32
BF16 = mybir.dt.bfloat16
U32 = mybir.dt.uint32
U8 = mybir.dt.uint8
FP8X4 = mybir.dt.float8_e4m3fn_x4
ALU = mybir.AluOpType
ACT = mybir.ActivationFunctionType
AX = mybir.AxisListType

B, C, T, H = 4, 512, 2048, 256
P = 128
PACK = 4
CHUNK = 512
NCH = T // CHUNK
TILES = CHUNK // P
NG = B * NCH
NQ = T // P
EPS_LN = 1e-5
EPS_STD = 1e-5
LEAD = 5
P4O = 2
RGA = 3
P4V_FROM = 12
BCS_AT = 1
VSQ = [14,15]
FLOPS = 2 * B * H * 3 * C * T


def tile_attentivestatspool_pa_t_kernel(tc, x, mask, w1, b1, g1, be1, out):
    nc = tc.nc
    with ExitStack() as ctx:
        const = ctx.enter_context(tc.tile_pool(name="const", bufs=1))
        xmp = ctx.enter_context(tc.tile_pool(name="xmp", bufs=3))
        grp = ctx.enter_context(tc.tile_pool(name="grp", bufs=6))
        cod = ctx.enter_context(tc.tile_pool(name="cod", bufs=3))
        sml = ctx.enter_context(tc.tile_pool(name="sml", bufs=6))
        per = ctx.enter_context(tc.tile_pool(name="per", bufs=2))
        up = ctx.enter_context(tc.tile_pool(name="up", bufs=5))
        zp = ctx.enter_context(tc.tile_pool(name="zp", bufs=3))
        op = ctx.enter_context(tc.tile_pool(name="op", bufs=3))
        ps_mx = ctx.enter_context(tc.psum_pool(name="ps_mx", bufs=3))
        ps_tr = ctx.enter_context(tc.psum_pool(name="ps_tr", bufs=3))
        ps_ms = ctx.enter_context(tc.psum_pool(name="ps_ms", bufs=1))
        ps_mk = ctx.enter_context(tc.psum_pool(name="ps_mk", bufs=1))
        ctx.enter_context(tc.manual_schedule())

        raw = [const.tile([P, PACK, T], BF16, name="raw%d" % b) for b in range(B)]
        w1_sb = const.tile([P, 2, 3 * C], BF16, name="w1_sb")
        pr = const.tile([P, P], BF16, name="pr")
        nc.vector.memset(pr[:], 0.0)
        x_v = [x[b].rearrange("(p j) t -> p j t", j=PACK) for b in range(B)]
        nc.scalar.dma_start(out=pr[0:B * NQ, :], in_=mask.rearrange("b o (q r) -> (b o q) r", r=P))
        nc.scalar.dma_start(out=pr[64:66, :], in_=g1.rearrange("(r f) -> r f", f=P))
        nc.scalar.dma_start(out=pr[66:68, :], in_=be1.rearrange("(r f) -> r f", f=P))
        nc.scalar.dma_start(out=pr[68:70, :], in_=b1.rearrange("(r f) -> r f", f=P))
        for s in range(NCH):
            nc.sync.dma_start(out=raw[0][:, :, s * CHUNK:(s + 1) * CHUNK],
                              in_=x_v[0][:, :, s * CHUNK:(s + 1) * CHUNK])
        nc.sync.dma_start(out=w1_sb[:], in_=w1.rearrange("(hh p) k -> p hh k", p=P))
        for b in range(1, B):
            nc.sync.dma_start(out=raw[b][:], in_=x_v[b])

        ident_b = const.tile([P, P], BF16, name="ident_b")
        make_identity(nc, ident_b[:])
        ident_f = const.tile([P, P], F32, name="ident_f")
        make_identity(nc, ident_f[:])
        ones_f = const.tile([P, P], F32, name="ones_f")
        nc.vector.memset(ones_f[:], 1.0)
        half = const.tile([P, PACK], F32, name="half")
        nc.vector.memset(half[:], 0.5)
        nhalf = const.tile([P, TILES], F32, name="nhalf")
        nc.vector.memset(nhalf[:], -0.5)
        rhs_tot = const.tile([P, 32], F32, name="rhs_tot")
        nc.vector.memset(rhs_tot[:], 0.0)

        w1c = const.tile([P, 3, H], U32, name="w1c", align_bytes=64)
        w1s = const.tile([P, 3, H], U8, name="w1s", align_bytes=64)
        w1p = const.tile([P, 2, 3, PACK, P], BF16, name="w1p")
        w1g = const.tile([P, 3, H, PACK], BF16, name="w1g", align_bytes=64)
        cols = const.tile([P, 72], BF16, name="cols")
        gb = const.tile([P, 4], F32, name="gb")
        r_t = const.tile([P, B], F32, name="r_t")
        b1bc = const.tile([P, H], BF16, name="b1bc")

        def columns():
            ps_pr = ps_ms.tile([P, P], BF16, tag="ms", name="ps_pr")
            nc.tensor.transpose(out=ps_pr[:], in_=pr[:], identity=ident_b[:])
            nc.vector.tensor_copy(out=cols[:, 0:70], in_=ps_pr[:, 0:70])
            nc.vector.tensor_copy(out=gb[:], in_=ps_pr[:, 64:68])

        def totals():
            nc.vector.tensor_reduce(out=rhs_tot[:, 0:B], in_=cols[:, 0:B * NQ].rearrange("p (b q) -> p b q", b=B),
                                    axis=AX.X, op=ALU.add)
            ps_tot = ps_ms.tile([P, 32], F32, tag="ms", name="ps_tot")
            nc.tensor.matmul(out=ps_tot[:], lhsT=ones_f[:], rhs=rhs_tot[:], start=True, stop=True)
            rtot = const.tile([P, B], F32, name="rtot")
            nc.vector.reciprocal(out=rtot[:], in_=ps_tot[:, 0:B])
            nc.vector.tensor_scalar(out=r_t[:], in0=rtot[:], scalar1=float(T), scalar2=None, op0=ALU.mult)
            ps_b1 = ps_ms.tile([P, H], BF16, tag="ms", name="ps_b1")
            for hh in range(2):
                nc.tensor.transpose(out=ps_b1[:, hh * P:(hh + 1) * P],
                                    in_=cols[:, 68 + hh:69 + hh].to_broadcast([P, P]), identity=ident_b[:])
            nc.vector.tensor_copy(out=b1bc[:], in_=ps_b1[:])

        def w1_permute():
            for hh in range(2):
                nc.scalar.copy(out=w1p[:, hh], in_=w1_sb[:, hh, :].rearrange("p (g q j) -> p g j q", g=3, j=PACK))

        def w1_transpose():
            for g in range(3):
                pw = ps_tr.tile([P, PACK, H], BF16, tag="tr", name="pw")
                for hh in range(2):
                    for j in range(PACK):
                        nc.tensor.transpose(out=pw[:, j, hh * P:(hh + 1) * P], in_=w1p[:, hh, g, j, :],
                                            identity=ident_b[:])
                nc.scalar.copy(out=w1g[:, g], in_=pw[:].rearrange("q j h -> q h j"))

        def w1_quant():
            for g in range(3):
                nc.vector.quantize_mx(out=w1c[:, g, :].bitcast(FP8X4), scales=w1s[:, g, :],
                                      in_=w1g[:, g].rearrange("q h j -> q (h j)"))

        xc = {}
        xs = {}
        st = {}
        vb = {}
        gr = {}
        mk = {}
        fin = {}

        def mask_bc(f):
            b, s = divmod(f, NCH)
            pmk = ps_mk.tile([P, CHUNK], BF16, name="pmk")
            for k in range(TILES):
                c = b * NQ + s * TILES + k
                nc.tensor.transpose(out=pmk[:, k * P:(k + 1) * P], in_=cols[:, c:c + 1].to_broadcast([P, P]),
                                    identity=ident_b[:])
            mk[f] = pmk

        def tt_bn(f, between):
            b, s = divmod(f, NCH)
            cols_f = slice(s * CHUNK, (s + 1) * CHUNK)
            if s == 0:
                st[b] = per.tile([P, PACK, NCH, 6], F32, name="st")
            xm = xmp.tile([P, PACK, CHUNK], BF16, name="xm")
            nc.vector.tensor_tensor(out=xm[:], in0=raw[b][:, :, cols_f],
                                    in1=mk.pop(f)[:].unsqueeze(1).to_broadcast([P, PACK, CHUNK]), op=ALU.mult)
            if f + 1 < NG:
                mask_bc(f + 1)
            for j in range(PACK):
                if j < len(between):
                    between[j]()
                nc.vector.bn_stats(out=st[b][:, j, s, :], in_=xm[:, j, :])

        def regroup(f):
            b, s = divmod(f, NCH)
            cols_f = slice(s * CHUNK, (s + 1) * CHUNK)
            grouped = grp.tile([P, CHUNK, PACK], BF16, name="grouped", align_bytes=64)
            nc.scalar.copy(out=grouped[:].rearrange("p (c i) j -> p c j i", i=4),
                           in_=raw[b][:, :, cols_f].rearrange("p j (c i) -> p c j i", i=4))
            gr[f] = grouped

        def quant(f):
            b, s = divmod(f, NCH)
            cols_f = slice(s * CHUNK, (s + 1) * CHUNK)
            if s == 0:
                xc[b] = cod.tile([P, T], U32, name="xc", align_bytes=64)
                xs[b] = cod.tile([P, T], U8, name="xs", align_bytes=64)
            nc.vector.quantize_mx(out=xc[b][:, cols_f].bitcast(FP8X4), scales=xs[b][:, cols_f],
                                  in_=gr.pop(f)[:].rearrange("p w j -> p (w j)"))

        def aggr(b):
            mv = per.tile([P, PACK, 2], F32, name="mv")
            for j in range(PACK):
                nc.vector.bn_aggr(out=mv[:, j, :], in_=st[b][:, j].rearrange("p s k -> p (s k)"))
            fin[b] = {"mv": mv}

        def stat_ops(b):
            e = fin[b]
            mean = e["mv"][:, :, 0]
            var = e["mv"][:, :, 1]
            rb = r_t[:, b:b + 1]
            m0 = per.tile([P, PACK], F32, name="m0")
            d = per.tile([P, PACK], F32, name="d")
            v0 = per.tile([P, PACK], F32, name="v0")
            e["m0"] = m0
            e["v0"] = v0
            return [
                lambda: nc.vector.tensor_scalar(out=m0[:], in0=mean, scalar1=rb, scalar2=None, op0=ALU.mult),
                lambda: nc.vector.tensor_tensor(out=d[:], in0=mean, in1=m0[:], op=ALU.subtract),
                lambda: nc.vector.tensor_tensor(out=d[:], in0=m0[:], in1=d[:], op=ALU.mult),
                lambda: nc.vector.scalar_tensor_tensor(out=v0[:], in0=var, scalar=rb, in1=d[:],
                                                       op0=ALU.mult, op1=ALU.add),
            ]

        def spread(b, gi, src):
            e = fin[b]
            msb = per.tile([P, P, PACK], BF16, name="msb%d" % gi, align_bytes=64)
            if b < B - 1:
                nc.gpsimd.tensor_scalar(out=msb[:], in0=src[:].unsqueeze(1).to_broadcast([P, P, PACK]),
                                        scalar1=1.0, scalar2=0.0, op0=ALU.mult, op1=ALU.add)
            else:
                nc.vector.tensor_copy(out=msb[:], in_=src[:].unsqueeze(1).to_broadcast([P, P, PACK]))
            e["msb%d" % gi] = msb

        def spread_q(b, gi):
            e = fin[b]
            msb = e["msb%d" % gi]
            mc = per.tile([P, P], U32, name="mc%d" % gi, align_bytes=64)
            msc = per.tile([P, P], U8, name="msc%d" % gi, align_bytes=64)
            nc.vector.quantize_mx(out=mc[:].bitcast(FP8X4), scales=msc[:], in_=msb[:].rearrange("p w j -> p (w j)"))
            if gi == 0:
                e["ps"] = ps_ms.tile([P, H], F32, tag="ms", name="ps_vb")
            nc.tensor.matmul_mx(out=e["ps"][:], lhsT=mc[:].bitcast(FP8X4), lhsT_scale=msc[:],
                                rhs=w1c[:, 1 + gi, :].bitcast(FP8X4), rhs_scale=w1s[:, 1 + gi, :],
                                start=(gi == 0), stop=(gi == 1))

        def stat_tail(b):
            e = fin[b]
            nc.vector.tensor_scalar(out=e["v0"][:], in0=e["v0"][:], scalar1=EPS_STD, scalar2=None, op0=ALU.max)
            std = per.tile([P, PACK], F32, name="std")
            nc.gpsimd.tensor_tensor(out=std[:], in0=e["v0"][:], in1=half[:], op=ALU.pow)
            e["std"] = std
            spread(b, 0, e["m0"])
            if b < B - 1:
                spread(b, 1, std)
            else:
                spread_q(b, 0)

        def vb_add(b):
            vb[b] = per.tile([P, H], F32, name="vb")
            nc.vector.tensor_tensor(out=vb[b][:], in0=fin.pop(b)["ps"][:], in1=b1bc[:], op=ALU.add)

        pss = {}
        av = {}
        sums = {}
        nrm = {}
        zhs = {}
        pts = {}

        def mx(g):
            b, s = divmod(g, NCH)
            pss[g] = []
            for pair in range(TILES // 2):
                ps = ps_mx.tile([P, 2, H], F32, name="ps")
                for i in range(2):
                    t0 = s * CHUNK + (2 * pair + i) * P
                    nc.tensor.matmul_mx(out=ps[:, i, :], lhsT=xc[b][:, t0:t0 + P].bitcast(FP8X4),
                                        lhsT_scale=xs[b][:, t0:t0 + P],
                                        rhs=w1c[:, 0, :].bitcast(FP8X4), rhs_scale=w1s[:, 0, :],
                                        start=True, stop=True)
                pss[g].append(ps)

        def p1(g):
            b = g // NCH
            a = up.tile([P, TILES, H], F32, name="a")
            for pair in range(TILES // 2):
                nc.vector.tensor_tensor(out=a[:, 2 * pair:2 * pair + 2, :], in0=pss[g][pair][:],
                                        in1=vb[b][:].unsqueeze(1).to_broadcast([P, 2, H]), op=ALU.add)
            pss.pop(g)
            av[g] = a
            if g in VSQ:
                s2v = sml.tile([P, TILES], F32, name="s2v")
                for k in range(TILES):
                    junkv = zp.tile([P, H], F32, name="junkv")
                    nc.vector.scalar_tensor_tensor(out=junkv[:], in0=a[:, k, :], scalar=0.0, in1=a[:, k, :],
                                                   op0=ALU.max, op1=ALU.mult, accum_out=s2v[:, k:k + 1])
                sums[(g, 1)] = s2v

        def relu(g):
            a = av[g]
            s1 = sml.tile([P, TILES], F32, name="s1")
            for k in range(TILES):
                nc.scalar.activation(out=a[:, k, :], in_=a[:, k, :], func=ACT.Relu, accum_out=s1[:, k:k + 1])
            sums[g] = s1

        def variance_s(g):
            a = av[g]
            negmu = sml.tile([P, TILES], F32, name="negmu")
            nc.scalar.activation(out=negmu[:], in_=sums.pop(g)[:], func=ACT.Copy, scale=-1.0 / H)
            nrm[g] = negmu
            if g not in VSQ:
                s2s = sml.tile([P, TILES], F32, name="s2s")
                for k in range(TILES):
                    junk = zp.tile([P, H], F32, name="junk")
                    nc.scalar.activation(out=junk[:], in_=a[:, k, :], func=ACT.Square, bias=negmu[:, k:k + 1],
                                         accum_out=s2s[:, k:k + 1])
                ve = sml.tile([P, TILES], F32, name="ve")
                nc.scalar.activation(out=ve[:], in_=s2s[:], func=ACT.Copy, scale=1.0 / H, bias=EPS_LN)
                rsqrt(g, ve)

        def variance_v(g):
            negmu = nrm[g]
            msq = sml.tile([P, TILES], F32, name="msq")
            vev = sml.tile([P, TILES], F32, name="vev")
            nc.vector.tensor_tensor(out=msq[:], in0=negmu[:], in1=negmu[:], op=ALU.mult)
            nc.vector.scalar_tensor_tensor(out=vev[:], in0=sums.pop((g, 1))[:], scalar=1.0 / H, in1=msq[:],
                                           op0=ALU.mult, op1=ALU.subtract)
            nc.vector.tensor_scalar(out=vev[:], in0=vev[:], scalar1=0.0, scalar2=EPS_LN, op0=ALU.max, op1=ALU.add)
            rsqrt(g, vev)

        def rsqrt(g, ve):
            rstd = sml.tile([P, TILES], F32, name="rstd")
            nc.gpsimd.tensor_tensor(out=rstd[:], in0=ve[:], in1=nhalf[:], op=ALU.pow)
            nrm[g] = (nrm[g], rstd)
            if g < P4V_FROM:
                normalise(g, nc.gpsimd)

        def normalise(g, eng):
            a = av.pop(g)
            negmu, rstd = nrm.pop(g)
            zh = zp.tile([P, TILES, H], F32, name="zh")
            for k in range(TILES):
                eng.tensor_scalar(out=zh[:, k, :], in0=a[:, k, :], scalar1=negmu[:, k:k + 1],
                                  scalar2=rstd[:, k:k + 1], op0=ALU.add, op1=ALU.mult)
            zhs[g] = zh

        def p4(g):
            zh = zhs.pop(g)
            pts[g] = []
            for hh in range(2):
                pt = ps_tr.tile([P, CHUNK], F32, tag="tr", name="pt")
                for k in range(TILES):
                    nc.tensor.transpose(out=pt[:, k * P:(k + 1) * P], in_=zh[:, k, hh * P:(hh + 1) * P],
                                        identity=ident_f[:])
                pts[g].append(pt)

        def tanh_store(g):
            b, s = divmod(g, NCH)
            o = op.tile([P, 2, CHUNK], F32, name="o")
            for hh in range(2):
                nc.scalar.activation(out=o[:, hh, :], in_=pts[g][hh][:], func=ACT.Tanh,
                                     scale=gb[:, hh:hh + 1], bias=gb[:, 2 + hh:3 + hh])
                if g == NG - 1:
                    nc.sync.dma_start(out=out[b][hh * P:(hh + 1) * P, s * CHUNK:(s + 1) * CHUNK], in_=o[:, hh, :])
            pts.pop(g)
            if g < NG - 1:
                nc.sync.dma_start(out=out[b].rearrange("(hh p) t -> p hh t", p=P)[:, :, s * CHUNK:(s + 1) * CHUNK],
                                  in_=o[:])

        def ok(g):
            return 0 <= g < NG

        def closed(f, k):
            return (f - k) // NCH if ok(f - k) and (f - k) % NCH == NCH - 1 else -1

        columns()
        mask_bc(0)
        done = {"rg": 0, "q": 0}
        rg_step = {}
        for i in range(-LEAD, NG + P4O + 2):
            f = i + LEAD
            b_1 = closed(f, 1)
            between = stat_ops(b_1) if b_1 >= 0 else []
            if 0 <= closed(f, 2) < B - 1:
                b_2 = closed(f, 2)
                between = [lambda: None, lambda: None, lambda: spread_q(b_2, 0), lambda: spread_q(b_2, 1)]
            if ok(f):
                tt_bn(f, between)
            else:
                for fn in between:
                    fn()
            if b_1 >= 0:
                stat_tail(b_1)
            if f == 1:
                totals()
            if closed(f, 0) >= 0:
                aggr(closed(f, 0))
            if ok(i + 1):
                mx(i + 1)
            if closed(f, BCS_AT + 1) >= 0:
                vb_add(closed(f, BCS_AT + 1))
            if ok(i):
                p1(i)
            if ok(i - 2) and (i - 2) in VSQ:
                variance_v(i - 2)
            if ok(i - 2) and i - 2 >= P4V_FROM:
                normalise(i - 2, nc.vector)
            if f == 3:
                w1_quant()
            while done["q"] < done["rg"] and rg_step[done["q"]] < i:
                quant(done["q"])
                done["q"] = done["q"] + 1
            if b_1 == B - 1:
                spread(b_1, 1, fin[b_1]["std"])
                spread_q(b_1, 1)
            if ok(i - 1):
                relu(i - 1)
                variance_s(i - 1)
            if ok(i - P4O):
                p4(i - P4O)
            if f == 1:
                w1_permute()
            if f == 2:
                w1_transpose()
            while done["rg"] <= min(NG - 1, f + RGA):
                regroup(done["rg"])
                rg_step[done["rg"]] = i
                done["rg"] = done["rg"] + 1
            if ok(i - P4O - 1):
                tanh_store(i - P4O - 1)
